import numpy as np
import ml_dtypes


def mxq(x, axis, fmt="e4m3"):
    dtype, down = {"e4m3": (ml_dtypes.float8_e4m3fn, 7), "e5m2": (ml_dtypes.float8_e5m2, 14)}[fmt]
    v = np.moveaxis(np.asarray(x, np.float32).astype(ml_dtypes.bfloat16).astype(np.float64), axis, -1)
    blocks = v.reshape(v.shape[:-1] + (-1, 32))
    amax = np.abs(blocks).max(-1, keepdims=True)
    byte = np.maximum(np.where(amax > 0, np.frexp(amax)[1] - 1 + 127, 0) - down, 1)
    scale = np.exp2(byte - 127.0)
    codes = (blocks / scale).astype(np.float32).astype(dtype).astype(np.float64)
    return np.moveaxis((codes * scale).reshape(v.shape), -1, axis)


WIDE = False


def mx_kscale(k):
    if not WIDE:
        return np.ones(k)
    levels = np.array([10, -10, 5, -5, 0])
    a = np.random.permutation(np.resize(levels, k // 512 * 4)).reshape(k // 512, 4)
    idx = np.arange(k)
    return np.exp2(a[idx // 512, idx % 128 // 32])


BF16 = ml_dtypes.bfloat16


def bf(x):
    return np.asarray(x, np.float32).astype(BF16)


def f64(x):
    return np.asarray(x).astype(np.float64)


E2M1 = np.array([0.0, 0.5, 1.0, 1.5, 2.0, 3.0, 4.0, 6.0, -0.0, -0.5, -1.0, -1.5, -2.0, -3.0, -4.0, -6.0])


def pack_weight(w, fmt):
    k, n = w.shape
    w = f64(bf(w)).reshape(k // 32, 32, n)
    amax = np.abs(w).max(1)
    if fmt == "e4m3":
        byte = np.frexp(amax)[1] - 1 + 127 - 7
    else:
        mant, ex = np.frexp(amax / 6.0)
        byte = np.where(mant > 0.5, ex, ex - 1) + 127
    byte = np.clip(np.where(amax > 0, byte, 1), 1, 254)
    scaled = (w * np.exp2(127.0 - byte)[:, None, :]).reshape(k, n).astype(np.float32)
    by_word = np.ascontiguousarray(scaled.reshape(k // 512, 128, 4, n).transpose(0, 1, 3, 2))
    if fmt == "e4m3":
        words = by_word.astype(ml_dtypes.float8_e4m3fn).view(np.uint8)
    else:
        c = by_word.astype(ml_dtypes.float4_e2m1fn).view(np.uint8) & 0xF
        words = c[..., 0::2] | (c[..., 1::2] << 4)
    return np.ascontiguousarray(words), np.ascontiguousarray(byte.astype(np.uint8).reshape(k // 512, 16, n))


def unpack_weight(words, scales, fmt):
    g, p, n, _ = words.shape
    if fmt == "e4m3":
        vals = np.ascontiguousarray(words).view(ml_dtypes.float8_e4m3fn).astype(np.float64)
    else:
        nib = np.empty((g, p, n, 4), np.uint8)
        nib[..., 0::2] = words & 0xF
        nib[..., 1::2] = words >> 4
        vals = E2M1[nib]
    vals = vals * np.repeat(np.exp2(scales.astype(np.float64) - 127.0), 8, axis=1)[..., None]
    return vals.transpose(0, 1, 3, 2).reshape(g * 512, n)

def pack4(w):
    words, scales = pack_weight(w, "e2m1")
    return words.reshape(words.shape[0], 128, -1), scales


def unpack4(words, scales):
    return unpack_weight(words.reshape(words.shape[0], 128, -1, 2), scales, "e2m1")


B, N, K, H, C_E, M = 2, 64, 16, 1024, 1024, 1024
SCALE = 30.0


def setup_inputs():
    s = mx_kscale(M)
    h2 = bf(np.random.standard_normal((B, N, K, M)) * 0.65 * s)
    h_V = bf(np.random.standard_normal((B, N, H)))
    mask_attend = bf(np.random.uniform(size=(B, N, K)) < 0.9)
    words, scales = pack4(np.random.standard_normal((M, H)) * 4.0 / np.sqrt(M) / s[:, None])
    W3_b = bf(np.random.standard_normal(H) * 0.1)
    return {"h2": h2,
            "h_V": h_V,
            "mask_attend": mask_attend,
            "W3_w_words": words,
            "W3_w_scales": scales,
            "W3_b": W3_b}


def reference(h2, h_V, mask_attend, W3_w_words, W3_w_scales, W3_b):
    h_message = (mxq(f64(h2), 3, "e4m3") @ unpack4(W3_w_words, W3_w_scales)) + f64(W3_b)
    h_message = f64(mask_attend)[..., None] * h_message
    dh = np.sum(h_message, axis=-2) / SCALE
    return f64(h_V) + dh

@@ -1,0 +1,145 @@
+from contextlib import ExitStack
+
+import concourse.mybir as mybir
+from concourse.masks import make_identity
+
+F32 = mybir.dt.float32
+BF16 = mybir.dt.bfloat16
+I32 = mybir.dt.int32
+U32 = mybir.dt.uint32
+U8 = mybir.dt.uint8
+FP8X4 = mybir.dt.float8_e4m3fn_x4
+FP4X4 = mybir.dt.float4_e2m1fn_x4
+MULT = mybir.AluOpType.mult
+ADD = mybir.AluOpType.add
+
+P = 128
+EDGES = 16
+M_IN = 1024
+H_OUT = 1024
+SCALE = 30.0
+PACK = 4
+K_PASS = P * PACK
+PASSES = M_IN // K_PASS
+HALVES = 2
+N_TILE = 512
+N_TILES = H_OUT // N_TILE
+GROUP = 4
+PAIR = 2
+
+FLOPS = 2 * P * EDGES * M_IN * H_OUT
+
+
+def tile_declayerj_pb_kernel(tc, h2, h_V, mask_attend, W3_w_words, W3_w_scales, W3_b, out):
+    nc = tc.nc
+    h2_by_node = h2.rearrange("b n k m -> (b n) k m")
+    mask_by_node = mask_attend.rearrange("b n k -> (b n) k")
+    hv_by_node = h_V.rearrange("b n h -> (b n) h")
+    out_by_node = out.rearrange("b n h -> (b n) h")
+
+    with ExitStack() as ctx:
+        keep = ctx.enter_context(tc.tile_pool(name="keep", bufs=1))
+        stage = ctx.enter_context(tc.tile_pool(name="stage", bufs=2))
+        sums = ctx.enter_context(tc.psum_pool(name="sums", bufs=1))
+        flips = ctx.enter_context(tc.psum_pool(name="flips", bufs=6))
+        ctx.enter_context(tc.manual_schedule())
+
+        mask = keep.tile([P, EDGES], BF16)
+        x = keep.tile([P, EDGES, M_IN], BF16)
+        w_words = keep.tile([P, PASSES, 2 * H_OUT], U8, align_bytes=64)
+        w_scales = keep.tile([P, PASSES, H_OUT], U8, align_bytes=64)
+        ident = keep.tile([P, P], F32)
+        masked_ident = keep.tile([P, EDGES, P], F32)
+        x_codes = keep.tile([P, EDGES, PASSES, P], U32, align_bytes=64)
+        x_scales = keep.tile([P, EDGES, PASSES, P], U8, align_bytes=64)
+        hv = keep.tile([P, H_OUT], BF16)
+        bias = keep.tile([P, H_OUT], BF16)
+        kept_edges = keep.tile([P, 1], F32)
+        bias_weight = keep.tile([P, 1], F32)
+        base = keep.tile([P, H_OUT], F32)
+        result = keep.tile([P, H_OUT], F32)
+        acc = [sums.tile([P, N_TILE], F32, name="acc%d" % n) for n in range(N_TILES)]
+
+        nc.vector.memset(w_scales[:].rearrange("p g n -> p (g n)").bitcast(I32), 0)
+        make_identity(nc, ident[:])
+
+        def load_edges(first, last):
+            for k in range(first, last):
+                nc.sync.dma_start(out=x[:, k, :], in_=h2_by_node[:, k, :])
+
+        nc.sync.dma_start(out=mask[:], in_=mask_by_node)
+        load_edges(0, GROUP)
+        for quadrant in range(4):
+            nc.sync.dma_start(
+                out=w_scales[32 * quadrant : 32 * quadrant + 4, :, :].bitcast(I32),
+                in_=W3_w_scales.bitcast(I32)[:, 4 * quadrant : 4 * quadrant + 4, :].rearrange("g r n -> r g n"),
+            )
+        for g in range(PASSES):
+            nc.sync.dma_start(out=w_words[:, g, :].bitcast(I32), in_=W3_w_words[g].bitcast(I32))
+        load_edges(GROUP, EDGES)
+        nc.sync.dma_start(out=hv[:], in_=hv_by_node)
+        nc.sync.dma_start(out=bias[:], in_=W3_b.partition_broadcast(P))
+
+        for k in range(EDGES):
+            nc.vector.tensor_scalar(
+                out=masked_ident[:, k, :], in0=ident[:], scalar1=mask[:, k : k + 1], scalar2=None, op0=MULT
+            )
+
+        x_words = x[:].bitcast(F32)
+
+        def transpose_and_quantise(first):
+            grouped = stage.tile([P, GROUP, PASSES, P, PACK], BF16, align_bytes=64)
+            grouped_words = grouped[:].bitcast(F32)
+            for i in range(GROUP):
+                k = first + i
+                flipped = flips.tile([P, PASSES, HALVES, P], F32)
+                for g in range(PASSES):
+                    for u in range(HALVES):
+                        nc.tensor.transpose(
+                            flipped[:, g, u, :],
+                            x_words[:, k, (K_PASS // 2) * g + u : (K_PASS // 2) * (g + 1) : HALVES],
+                            masked_ident[:, k, :],
+                        )
+                copy = nc.vector.tensor_copy if i % 2 == 0 else nc.scalar.copy
+                copy(out=grouped_words[:, i], in_=flipped[:].rearrange("p g u n -> p g n u"))
+            for i in range(0, GROUP, PAIR):
+                k = first + i
+                nc.vector.quantize_mx(
+                    out=x_codes[:, k : k + PAIR].rearrange("p k g n -> p (k g n)").bitcast(FP8X4),
+                    scales=x_scales[:, k : k + PAIR].rearrange("p k g n -> p (k g n)"),
+                    in_=grouped[:, i : i + PAIR].rearrange("p k g n t -> p (k g n t)"),
+                )
+
+        def multiply(first):
+            for n in range(N_TILES):
+                for k in range(first, first + GROUP):
+                    for g in range(PASSES):
+                        nc.tensor.matmul_mx(
+                            out=acc[n][:],
+                            lhsT=x_codes[:, k, g, :].bitcast(FP8X4),
+                            lhsT_scale=x_scales[:, k, g, :],
+                            rhs=w_words[:, g, 2 * N_TILE * n : 2 * N_TILE * (n + 1)].bitcast(FP4X4),
+                            rhs_scale=w_scales[:, g, N_TILE * n : N_TILE * (n + 1)],
+                            start=(k == 0 and g == 0),
+                            stop=(k == EDGES - 1 and g == PASSES - 1),
+                        )
+
+        transpose_and_quantise(0)
+        for first in range(GROUP, EDGES, GROUP):
+            transpose_and_quantise(first)
+            multiply(first - GROUP)
+
+        nc.vector.tensor_reduce(out=kept_edges[:], in_=mask[:], axis=mybir.AxisListType.X, op=ADD)
+        nc.vector.tensor_scalar(out=bias_weight[:], in0=kept_edges[:], scalar1=1.0 / SCALE, scalar2=None, op0=MULT)
+        nc.vector.scalar_tensor_tensor(
+            out=base[:], in0=bias[:], scalar=bias_weight[:, 0:1], in1=hv[:], op0=MULT, op1=ADD
+        )
+
+        multiply(EDGES - GROUP)
+
+        for n in range(N_TILES):
+            cols = slice(N_TILE * n, N_TILE * (n + 1))
+            nc.vector.scalar_tensor_tensor(
+                out=result[:, cols], in0=acc[n][:], scalar=1.0 / SCALE, in1=base[:, cols], op0=MULT, op1=ADD
+            )
+            nc.sync.dma_start(out=out_by_node[:, cols], in_=result[:, cols])

@@ -50,6 +50,7 @@ def tile_declayerj_pb_kernel(tc, h2, h_V, mask_attend, W3_w_words, W3_w_scales, 
         w_scales = keep.tile([P, PASSES, H_OUT], U8, align_bytes=64)
         ident = keep.tile([P, P], F32)
         masked_ident = keep.tile([P, EDGES, P], F32)
+        x_sorted = keep.tile([P, EDGES, PASSES, HALVES, P], F32)
         x_codes = keep.tile([P, EDGES, PASSES, P], U32, align_bytes=64)
         x_scales = keep.tile([P, EDGES, PASSES, P], U8, align_bytes=64)
         hv = keep.tile([P, H_OUT], BF16)
@@ -80,11 +81,6 @@ def tile_declayerj_pb_kernel(tc, h2, h_V, mask_attend, W3_w_words, W3_w_scales, 
         nc.sync.dma_start(out=hv[:], in_=hv_by_node)
         nc.sync.dma_start(out=bias[:], in_=W3_b.partition_broadcast(P))
 
-        for k in range(EDGES):
-            nc.vector.tensor_scalar(
-                out=masked_ident[:, k, :], in0=ident[:], scalar1=mask[:, k : k + 1], scalar2=None, op0=MULT
-            )
-
         x_words = x[:].bitcast(F32)
 
         def transpose_and_quantise(first):
@@ -92,16 +88,18 @@ def tile_declayerj_pb_kernel(tc, h2, h_V, mask_attend, W3_w_words, W3_w_scales, 
             grouped_words = grouped[:].bitcast(F32)
             for i in range(GROUP):
                 k = first + i
+                nc.vector.tensor_scalar(
+                    out=masked_ident[:, k, :], in0=ident[:], scalar1=mask[:, k : k + 1], scalar2=None, op0=MULT
+                )
+                nc.vector.tensor_copy(
+                    out=x_sorted[:, k],
+                    in_=x_words[:, k, :].rearrange("p (g q u) -> p g u q", g=PASSES, u=HALVES),
+                )
                 flipped = flips.tile([P, PASSES, HALVES, P], F32)
                 for g in range(PASSES):
                     for u in range(HALVES):
-                        nc.tensor.transpose(
-                            flipped[:, g, u, :],
-                            x_words[:, k, (K_PASS // 2) * g + u : (K_PASS // 2) * (g + 1) : HALVES],
-                            masked_ident[:, k, :],
-                        )
-                copy = nc.vector.tensor_copy if i % 2 == 0 else nc.scalar.copy
-                copy(out=grouped_words[:, i], in_=flipped[:].rearrange("p g u n -> p g n u"))
+                        nc.tensor.transpose(flipped[:, g, u, :], x_sorted[:, k, g, u, :], masked_ident[:, k, :])
+                nc.scalar.copy(out=grouped_words[:, i], in_=flipped[:].rearrange("p g u n -> p g n u"))
             for i in range(0, GROUP, PAIR):
                 k = first + i
                 nc.vector.quantize_mx(
@@ -110,24 +108,24 @@ def tile_declayerj_pb_kernel(tc, h2, h_V, mask_attend, W3_w_words, W3_w_scales, 
                     in_=grouped[:, i : i + PAIR].rearrange("p k g n t -> p (k g n t)"),
                 )
 
-        def multiply(first):
-            for n in range(N_TILES):
-                for k in range(first, first + GROUP):
-                    for g in range(PASSES):
-                        nc.tensor.matmul_mx(
-                            out=acc[n][:],
-                            lhsT=x_codes[:, k, g, :].bitcast(FP8X4),
-                            lhsT_scale=x_scales[:, k, g, :],
-                            rhs=w_words[:, g, 2 * N_TILE * n : 2 * N_TILE * (n + 1)].bitcast(FP4X4),
-                            rhs_scale=w_scales[:, g, N_TILE * n : N_TILE * (n + 1)],
-                            start=(k == 0 and g == 0),
-                            stop=(k == EDGES - 1 and g == PASSES - 1),
-                        )
+        def multiply(first, n):
+            for k in range(first, first + GROUP):
+                for g in range(PASSES):
+                    nc.tensor.matmul_mx(
+                        out=acc[n][:],
+                        lhsT=x_codes[:, k, g, :].bitcast(FP8X4),
+                        lhsT_scale=x_scales[:, k, g, :],
+                        rhs=w_words[:, g, 2 * N_TILE * n : 2 * N_TILE * (n + 1)].bitcast(FP4X4),
+                        rhs_scale=w_scales[:, g, N_TILE * n : N_TILE * (n + 1)],
+                        start=(k == 0 and g == 0),
+                        stop=(k == EDGES - 1 and g == PASSES - 1),
+                    )
 
         transpose_and_quantise(0)
         for first in range(GROUP, EDGES, GROUP):
+            multiply(first - GROUP, 0)
             transpose_and_quantise(first)
-            multiply(first - GROUP)
+            multiply(first - GROUP, 1)
 
         nc.vector.tensor_reduce(out=kept_edges[:], in_=mask[:], axis=mybir.AxisListType.X, op=ADD)
         nc.vector.tensor_scalar(out=bias_weight[:], in0=kept_edges[:], scalar1=1.0 / SCALE, scalar2=None, op0=MULT)
@@ -135,7 +133,8 @@ def tile_declayerj_pb_kernel(tc, h2, h_V, mask_attend, W3_w_words, W3_w_scales, 
             out=base[:], in0=bias[:], scalar=bias_weight[:, 0:1], in1=hv[:], op0=MULT, op1=ADD
         )
 
-        multiply(EDGES - GROUP)
+        multiply(EDGES - GROUP, 0)
+        multiply(EDGES - GROUP, 1)
 
         for n in range(N_TILES):
             cols = slice(N_TILE * n, N_TILE * (n + 1))

@@ -25,7 +25,6 @@ HALVES = 2
 N_TILE = 512
 N_TILES = H_OUT // N_TILE
 GROUP = 4
-PAIR = 2
 
 FLOPS = 2 * P * EDGES * M_IN * H_OUT
 
@@ -39,7 +38,7 @@ def tile_declayerj_pb_kernel(tc, h2, h_V, mask_attend, W3_w_words, W3_w_scales, 
 
     with ExitStack() as ctx:
         keep = ctx.enter_context(tc.tile_pool(name="keep", bufs=1))
-        stage = ctx.enter_context(tc.tile_pool(name="stage", bufs=2))
+        stage = ctx.enter_context(tc.tile_pool(name="stage", bufs=2 * GROUP))
         sums = ctx.enter_context(tc.psum_pool(name="sums", bufs=1))
         flips = ctx.enter_context(tc.psum_pool(name="flips", bufs=6))
         ctx.enter_context(tc.manual_schedule())
@@ -68,6 +67,12 @@ def tile_declayerj_pb_kernel(tc, h2, h_V, mask_attend, W3_w_words, W3_w_scales, 
             for k in range(first, last):
                 nc.sync.dma_start(out=x[:, k, :], in_=h2_by_node[:, k, :])
 
+        def load_weight_half(n):
+            nc.sync.dma_start(
+                out=w_words[:, :, 2 * N_TILE * n : 2 * N_TILE * (n + 1)].bitcast(I32),
+                in_=W3_w_words.bitcast(I32)[:, :, N_TILE // 2 * n : N_TILE // 2 * (n + 1)].rearrange("g p b -> p g b"),
+            )
+
         nc.sync.dma_start(out=mask[:], in_=mask_by_node)
         load_edges(0, GROUP)
         for quadrant in range(4):
@@ -75,19 +80,18 @@ def tile_declayerj_pb_kernel(tc, h2, h_V, mask_attend, W3_w_words, W3_w_scales, 
                 out=w_scales[32 * quadrant : 32 * quadrant + 4, :, :].bitcast(I32),
                 in_=W3_w_scales.bitcast(I32)[:, 4 * quadrant : 4 * quadrant + 4, :].rearrange("g r n -> r g n"),
             )
-        for g in range(PASSES):
-            nc.sync.dma_start(out=w_words[:, g, :].bitcast(I32), in_=W3_w_words[g].bitcast(I32))
-        load_edges(GROUP, EDGES)
+        load_weight_half(0)
+        load_edges(GROUP, 2 * GROUP)
+        load_weight_half(1)
+        load_edges(2 * GROUP, EDGES)
         nc.sync.dma_start(out=hv[:], in_=hv_by_node)
         nc.sync.dma_start(out=bias[:], in_=W3_b.partition_broadcast(P))
 
         x_words = x[:].bitcast(F32)
 
         def transpose_and_quantise(first):
-            grouped = stage.tile([P, GROUP, PASSES, P, PACK], BF16, align_bytes=64)
-            grouped_words = grouped[:].bitcast(F32)
-            for i in range(GROUP):
-                k = first + i
+            group_tiles = []
+            for k in range(first, first + GROUP):
                 nc.vector.tensor_scalar(
                     out=masked_ident[:, k, :], in0=ident[:], scalar1=mask[:, k : k + 1], scalar2=None, op0=MULT
                 )
@@ -99,13 +103,14 @@ def tile_declayerj_pb_kernel(tc, h2, h_V, mask_attend, W3_w_words, W3_w_scales, 
                 for g in range(PASSES):
                     for u in range(HALVES):
                         nc.tensor.transpose(flipped[:, g, u, :], x_sorted[:, k, g, u, :], masked_ident[:, k, :])
-                nc.scalar.copy(out=grouped_words[:, i], in_=flipped[:].rearrange("p g u n -> p g n u"))
-            for i in range(0, GROUP, PAIR):
-                k = first + i
+                grouped = stage.tile([P, PASSES, P, PACK], BF16, align_bytes=64)
+                nc.scalar.copy(out=grouped[:].bitcast(F32), in_=flipped[:].rearrange("p g u n -> p g n u"))
+                group_tiles.append(grouped)
+            for k, grouped in zip(range(first, first + GROUP), group_tiles):
                 nc.vector.quantize_mx(
-                    out=x_codes[:, k : k + PAIR].rearrange("p k g n -> p (k g n)").bitcast(FP8X4),
-                    scales=x_scales[:, k : k + PAIR].rearrange("p k g n -> p (k g n)"),
-                    in_=grouped[:, i : i + PAIR].rearrange("p k g n t -> p (k g n t)"),
+                    out=x_codes[:, k].rearrange("p g n -> p (g n)").bitcast(FP8X4),
+                    scales=x_scales[:, k].rearrange("p g n -> p (g n)"),
+                    in_=grouped[:].rearrange("p g n t -> p (g n t)"),
                 )
 
         def multiply(first, n):

@@ -45,7 +45,7 @@ def tile_declayerj_pb_kernel(tc, h2, h_V, mask_attend, W3_w_words, W3_w_scales, 
 
         mask = keep.tile([P, EDGES], BF16)
         x = keep.tile([P, EDGES, M_IN], BF16)
-        w_words = keep.tile([P, PASSES, 2 * H_OUT], U8, align_bytes=64)
+        w_words = keep.tile([P, N_TILES, PASSES, 2 * N_TILE], U8, align_bytes=64)
         w_scales = keep.tile([P, PASSES, H_OUT], U8, align_bytes=64)
         ident = keep.tile([P, P], F32)
         masked_ident = keep.tile([P, EDGES, P], F32)
@@ -69,7 +69,7 @@ def tile_declayerj_pb_kernel(tc, h2, h_V, mask_attend, W3_w_words, W3_w_scales, 
 
         def load_weight_half(n):
             nc.sync.dma_start(
-                out=w_words[:, :, 2 * N_TILE * n : 2 * N_TILE * (n + 1)].bitcast(I32),
+                out=w_words[:, n].bitcast(I32),
                 in_=W3_w_words.bitcast(I32)[:, :, N_TILE // 2 * n : N_TILE // 2 * (n + 1)].rearrange("g p b -> p g b"),
             )
 
@@ -120,7 +120,7 @@ def tile_declayerj_pb_kernel(tc, h2, h_V, mask_attend, W3_w_words, W3_w_scales, 
                         out=acc[n][:],
                         lhsT=x_codes[:, k, g, :].bitcast(FP8X4),
                         lhsT_scale=x_scales[:, k, g, :],
-                        rhs=w_words[:, g, 2 * N_TILE * n : 2 * N_TILE * (n + 1)].bitcast(FP4X4),
+                        rhs=w_words[:, n, g, :].bitcast(FP4X4),
                         rhs_scale=w_scales[:, g, N_TILE * n : N_TILE * (n + 1)],
                         start=(k == 0 and g == 0),
                         stop=(k == EDGES - 1 and g == PASSES - 1),

@@ -25,6 +25,7 @@ HALVES = 2
 N_TILE = 512
 N_TILES = H_OUT // N_TILE
 GROUP = 4
+WARM_FIRST = 6
 
 FLOPS = 2 * P * EDGES * M_IN * H_OUT
 
@@ -40,7 +41,8 @@ def tile_declayerj_pb_kernel(tc, h2, h_V, mask_attend, W3_w_words, W3_w_scales, 
         keep = ctx.enter_context(tc.tile_pool(name="keep", bufs=1))
         stage = ctx.enter_context(tc.tile_pool(name="stage", bufs=2 * GROUP))
         sums = ctx.enter_context(tc.psum_pool(name="sums", bufs=1))
-        flips = ctx.enter_context(tc.psum_pool(name="flips", bufs=6))
+        flips = ctx.enter_context(tc.psum_pool(name="flips", bufs=5))
+        spare = ctx.enter_context(tc.psum_pool(name="spare", bufs=1))
         ctx.enter_context(tc.manual_schedule())
 
         mask = keep.tile([P, EDGES], BF16)
@@ -59,6 +61,16 @@ def tile_declayerj_pb_kernel(tc, h2, h_V, mask_attend, W3_w_words, W3_w_scales, 
         base = keep.tile([P, H_OUT], F32)
         result = keep.tile([P, H_OUT], F32)
         acc = [sums.tile([P, N_TILE], F32, name="acc%d" % n) for n in range(N_TILES)]
+        zeros = keep.tile([P, N_TILE], BF16)
+        unread = spare.tile([P, N_TILE], F32)
+
+        nc.vector.memset(zeros[:], 0.0)
+
+        def keep_warm(count):
+            for i in range(count):
+                nc.tensor.matmul(out=unread[:], lhsT=zeros[:, 0:P], rhs=zeros[:], start=True, stop=True)
+
+        keep_warm(WARM_FIRST)
 
         nc.vector.memset(w_scales[:].rearrange("p g n -> p (g n)").bitcast(I32), 0)
         make_identity(nc, ident[:])
@@ -103,6 +115,8 @@ def tile_declayerj_pb_kernel(tc, h2, h_V, mask_attend, W3_w_words, W3_w_scales, 
                 for g in range(PASSES):
                     for u in range(HALVES):
                         nc.tensor.transpose(flipped[:, g, u, :], x_sorted[:, k, g, u, :], masked_ident[:, k, :])
+                if first == 0:
+                    keep_warm(1)
                 grouped = stage.tile([P, PASSES, P, PACK], BF16, align_bytes=64)
                 nc.scalar.copy(out=grouped[:].bitcast(F32), in_=flipped[:].rearrange("p g u n -> p g n u"))
                 group_tiles.append(grouped)

@@ -26,6 +26,11 @@ N_TILE = 512
 N_TILES = H_OUT // N_TILE
 GROUP = 4
 WARM_FIRST = 6
+BY_VECTOR = 4
+BY_TENSOR = EDGES - BY_VECTOR
+QUADRANTS = 4
+Q = P // QUADRANTS
+COPY = mybir.ActivationFunctionType.Copy
 
 FLOPS = 2 * P * EDGES * M_IN * H_OUT
 
@@ -46,7 +51,12 @@ def tile_declayerj_pb_kernel(tc, h2, h_V, mask_attend, W3_w_words, W3_w_scales, 
         ctx.enter_context(tc.manual_schedule())
 
         mask = keep.tile([P, EDGES], BF16)
-        x = keep.tile([P, EDGES, M_IN], BF16)
+        x = keep.tile([P, BY_TENSOR, M_IN], BF16)
+        a0 = keep.tile([P, QUADRANTS, BY_VECTOR, PASSES * Q * PACK], BF16, align_bytes=64)
+        a1 = keep.tile([P, BY_VECTOR, QUADRANTS, PASSES * Q * PACK], BF16, align_bytes=64)
+        t1 = keep.tile([P, BY_VECTOR, QUADRANTS * PASSES * Q * HALVES], F32, align_bytes=64)
+        mask_a_bf = keep.tile([P, QUADRANTS, EDGES], BF16)
+        mask_a = keep.tile([P, QUADRANTS, EDGES], F32)
         w_words = keep.tile([P, N_TILES, PASSES, 2 * N_TILE], U8, align_bytes=64)
         w_scales = keep.tile([P, PASSES, H_OUT], U8, align_bytes=64)
         ident = keep.tile([P, P], F32)
@@ -95,7 +105,19 @@ def tile_declayerj_pb_kernel(tc, h2, h_V, mask_attend, W3_w_words, W3_w_scales, 
         load_weight_half(0)
         load_edges(GROUP, 2 * GROUP)
         load_weight_half(1)
-        load_edges(2 * GROUP, EDGES)
+        load_edges(2 * GROUP, BY_TENSOR)
+        for q in range(QUADRANTS):
+            nc.sync.dma_start(
+                out=mask_a_bf[Q * q : Q * (q + 1)], in_=mask_by_node.rearrange("(b j) k -> j b k", b=QUADRANTS)
+            )
+        for b in range(QUADRANTS):
+            for q in (0, 2, 1, 3):
+                nc.sync.dma_start(
+                    out=a0[Q * q : Q * (q + 1), b].rearrange("p v (g w) -> p (v g) w", g=PASSES),
+                    in_=h2_by_node[Q * b : Q * (b + 1), BY_TENSOR:EDGES, :].rearrange(
+                        "n v (g q w) -> n (v g) q w", g=PASSES, q=QUADRANTS
+                    )[:, :, q, :],
+                )
         nc.sync.dma_start(out=hv[:], in_=hv_by_node)
         nc.sync.dma_start(out=bias[:], in_=W3_b.partition_broadcast(P))
 
@@ -127,24 +149,60 @@ def tile_declayerj_pb_kernel(tc, h2, h_V, mask_attend, W3_w_words, W3_w_scales, 
                     in_=grouped[:].rearrange("p g n t -> p (g n t)"),
                 )
 
+        def multiply_edge(k, n):
+            for g in range(PASSES):
+                nc.tensor.matmul_mx(
+                    out=acc[n][:],
+                    lhsT=x_codes[:, k, g, :].bitcast(FP8X4),
+                    lhsT_scale=x_scales[:, k, g, :],
+                    rhs=w_words[:, n, g, :].bitcast(FP4X4),
+                    rhs_scale=w_scales[:, g, N_TILE * n : N_TILE * (n + 1)],
+                    start=(k == 0 and g == 0),
+                    stop=(k == EDGES - 1 and g == PASSES - 1),
+                )
+
         def multiply(first, n):
             for k in range(first, first + GROUP):
-                for g in range(PASSES):
-                    nc.tensor.matmul_mx(
-                        out=acc[n][:],
-                        lhsT=x_codes[:, k, g, :].bitcast(FP8X4),
-                        lhsT_scale=x_scales[:, k, g, :],
-                        rhs=w_words[:, n, g, :].bitcast(FP4X4),
-                        rhs_scale=w_scales[:, g, N_TILE * n : N_TILE * (n + 1)],
-                        start=(k == 0 and g == 0),
-                        stop=(k == EDGES - 1 and g == PASSES - 1),
-                    )
+                multiply_edge(k, n)
 
         transpose_and_quantise(0)
-        for first in range(GROUP, EDGES, GROUP):
+        for first in range(GROUP, BY_TENSOR, GROUP):
             multiply(first - GROUP, 0)
             transpose_and_quantise(first)
             multiply(first - GROUP, 1)
+
+        nc.vector.tensor_copy(out=mask_a[:], in_=mask_a_bf[:])
+        for v in range(BY_VECTOR):
+            for b in range(QUADRANTS):
+                nc.scalar.activation(
+                    out=a1[:, v, b].rearrange("p (u i h) -> p u i h", u=HALVES, h=2),
+                    in_=a0[:, b, v].rearrange("p (i u h) -> p u i h", u=HALVES, h=2),
+                    func=COPY,
+                    scale=mask_a[:, b, BY_TENSOR + v : BY_TENSOR + v + 1],
+                )
+
+        def flip_blocks(v):
+            nc.vector.transpose(out=t1[:, v, :], in_=a1[:, v].rearrange("p b c -> p (b c)").bitcast(F32))
+
+        flip_blocks(0)
+        for v in range(BY_VECTOR):
+            k = BY_TENSOR + v
+            grouped = stage.tile([P, PASSES, P, PACK], BF16, align_bytes=64)
+            for g in range(PASSES):
+                nc.vector.tensor_copy(
+                    out=grouped[:, g]
+                    .rearrange("p n t -> p (n t)")
+                    .bitcast(F32)
+                    .rearrange("p (b j u) -> p b j u", b=QUADRANTS, u=HALVES),
+                    in_=t1[:, v].rearrange("p (b u g j) -> p g b j u", b=QUADRANTS, u=HALVES, g=PASSES)[:, g],
+                )
+            if v + 1 < BY_VECTOR:
+                flip_blocks(v + 1)
+            nc.vector.quantize_mx(
+                out=x_codes[:, k].rearrange("p g n -> p (g n)").bitcast(FP8X4),
+                scales=x_scales[:, k].rearrange("p g n -> p (g n)"),
+                in_=grouped[:].rearrange("p g n t -> p (g n t)"),
+            )
 
         nc.vector.tensor_reduce(out=kept_edges[:], in_=mask[:], axis=mybir.AxisListType.X, op=ADD)
         nc.vector.tensor_scalar(out=bias_weight[:], in0=kept_edges[:], scalar1=1.0 / SCALE, scalar2=None, op0=MULT)
@@ -152,8 +210,14 @@ def tile_declayerj_pb_kernel(tc, h2, h_V, mask_attend, W3_w_words, W3_w_scales, 
             out=base[:], in0=bias[:], scalar=bias_weight[:, 0:1], in1=hv[:], op0=MULT, op1=ADD
         )
 
-        multiply(EDGES - GROUP, 0)
-        multiply(EDGES - GROUP, 1)
+        multiply(BY_TENSOR - GROUP, 0)
+        multiply(BY_TENSOR - GROUP, 1)
+        for k in range(BY_TENSOR, EDGES - 2):
+            for n in range(N_TILES):
+                multiply_edge(k, n)
+        for n in range(N_TILES):
+            for k in range(EDGES - 2, EDGES):
+                multiply_edge(k, n)
 
         for n in range(N_TILES):
             cols = slice(N_TILE * n, N_TILE * (n + 1))

@@ -55,8 +55,8 @@ def tile_declayerj_pb_kernel(tc, h2, h_V, mask_attend, W3_w_words, W3_w_scales, 
         a0 = keep.tile([P, QUADRANTS, BY_VECTOR, PASSES * Q * PACK], BF16, align_bytes=64)
         a1 = keep.tile([P, BY_VECTOR, QUADRANTS, PASSES * Q * PACK], BF16, align_bytes=64)
         t1 = keep.tile([P, BY_VECTOR, QUADRANTS * PASSES * Q * HALVES], F32, align_bytes=64)
-        mask_a_bf = keep.tile([P, QUADRANTS, EDGES], BF16)
         mask_a = keep.tile([P, QUADRANTS, EDGES], F32)
+        pick = keep.tile([P, QUADRANTS, QUADRANTS, Q], BF16)
         w_words = keep.tile([P, N_TILES, PASSES, 2 * N_TILE], U8, align_bytes=64)
         w_scales = keep.tile([P, PASSES, H_OUT], U8, align_bytes=64)
         ident = keep.tile([P, P], F32)
@@ -95,6 +95,15 @@ def tile_declayerj_pb_kernel(tc, h2, h_V, mask_attend, W3_w_words, W3_w_scales, 
                 in_=W3_w_words.bitcast(I32)[:, :, N_TILE // 2 * n : N_TILE // 2 * (n + 1)].rearrange("g p b -> p g b"),
             )
 
+        def load_by_quadrant(pieces):
+            for b, q in pieces:
+                nc.sync.dma_start(
+                    out=a0[Q * q : Q * (q + 1), b].rearrange("p v (g w) -> p (v g) w", g=PASSES),
+                    in_=h2_by_node[Q * b : Q * (b + 1), BY_TENSOR:EDGES, :].rearrange(
+                        "n v (g q w) -> n (v g) q w", g=PASSES, q=QUADRANTS
+                    )[:, :, q, :],
+                )
+
         nc.sync.dma_start(out=mask[:], in_=mask_by_node)
         load_edges(0, GROUP)
         for quadrant in range(4):
@@ -105,49 +114,72 @@ def tile_declayerj_pb_kernel(tc, h2, h_V, mask_attend, W3_w_words, W3_w_scales, 
         load_weight_half(0)
         load_edges(GROUP, 2 * GROUP)
         load_weight_half(1)
+        pieces = [(b, q) for b in range(QUADRANTS) for q in (0, 2, 1, 3)]
+        load_by_quadrant(pieces[:QUADRANTS])
         load_edges(2 * GROUP, BY_TENSOR)
-        for q in range(QUADRANTS):
-            nc.sync.dma_start(
-                out=mask_a_bf[Q * q : Q * (q + 1)], in_=mask_by_node.rearrange("(b j) k -> j b k", b=QUADRANTS)
-            )
-        for b in range(QUADRANTS):
-            for q in (0, 2, 1, 3):
-                nc.sync.dma_start(
-                    out=a0[Q * q : Q * (q + 1), b].rearrange("p v (g w) -> p (v g) w", g=PASSES),
-                    in_=h2_by_node[Q * b : Q * (b + 1), BY_TENSOR:EDGES, :].rearrange(
-                        "n v (g q w) -> n (v g) q w", g=PASSES, q=QUADRANTS
-                    )[:, :, q, :],
-                )
+        load_by_quadrant(pieces[QUADRANTS:])
         nc.sync.dma_start(out=hv[:], in_=hv_by_node)
         nc.sync.dma_start(out=bias[:], in_=W3_b.partition_broadcast(P))
 
-        x_words = x[:].bitcast(F32)
+        for q in range(QUADRANTS):
+            nc.vector.tensor_copy(out=pick[:, :, q, :], in_=ident[:].rearrange("p (b j) -> p b j", b=QUADRANTS))
+        picked = flips.tile([P, QUADRANTS, EDGES], F32, name="flipped")
+        for b in range(QUADRANTS):
+            nc.tensor.matmul(
+                out=picked[:, b, :], lhsT=pick[:, b].rearrange("p q j -> p (q j)"), rhs=mask[:], start=True, stop=True
+            )
 
-        def transpose_and_quantise(first):
-            group_tiles = []
-            for k in range(first, first + GROUP):
-                nc.vector.tensor_scalar(
-                    out=masked_ident[:, k, :], in0=ident[:], scalar1=mask[:, k : k + 1], scalar2=None, op0=MULT
+        x_words = x[:].bitcast(F32)
+        staged = {}
+
+        def flip_on_tensor(k):
+            nc.vector.tensor_scalar(
+                out=masked_ident[:, k, :], in0=ident[:], scalar1=mask[:, k : k + 1], scalar2=None, op0=MULT
+            )
+            nc.vector.tensor_copy(
+                out=x_sorted[:, k],
+                in_=x_words[:, k, :].rearrange("p (g q u) -> p g u q", g=PASSES, u=HALVES),
+            )
+            flipped = flips.tile([P, PASSES, HALVES, P], F32)
+            for g in range(PASSES):
+                for u in range(HALVES):
+                    nc.tensor.transpose(flipped[:, g, u, :], x_sorted[:, k, g, u, :], masked_ident[:, k, :])
+            if k < GROUP:
+                keep_warm(1)
+            grouped = stage.tile([P, PASSES, P, PACK], BF16, align_bytes=64)
+            nc.scalar.copy(out=grouped[:].bitcast(F32), in_=flipped[:].rearrange("p g u n -> p g n u"))
+            staged[k] = grouped
+
+        def mask_and_sort(v):
+            for b in range(QUADRANTS):
+                nc.scalar.activation(
+                    out=a1[:, v, b].rearrange("p (u i h) -> p u i h", u=HALVES, h=2),
+                    in_=a0[:, b, v].rearrange("p (i u h) -> p u i h", u=HALVES, h=2),
+                    func=COPY,
+                    scale=mask_a[:, b, BY_TENSOR + v : BY_TENSOR + v + 1],
                 )
-                nc.vector.tensor_copy(
-                    out=x_sorted[:, k],
-                    in_=x_words[:, k, :].rearrange("p (g q u) -> p g u q", g=PASSES, u=HALVES),
+
+        def flip_blocks(v):
+            nc.vector.transpose(out=t1[:, v, :], in_=a1[:, v].rearrange("p b c -> p (b c)").bitcast(F32))
+
+        def interleave(v, copy):
+            grouped = stage.tile([P, PASSES, P, PACK], BF16, align_bytes=64)
+            for g in range(PASSES):
+                copy(
+                    out=grouped[:, g]
+                    .rearrange("p n t -> p (n t)")
+                    .bitcast(F32)
+                    .rearrange("p (b j u) -> p b j u", b=QUADRANTS, u=HALVES),
+                    in_=t1[:, v].rearrange("p (b u g j) -> p g b j u", b=QUADRANTS, u=HALVES, g=PASSES)[:, g],
                 )
-                flipped = flips.tile([P, PASSES, HALVES, P], F32)
-                for g in range(PASSES):
-                    for u in range(HALVES):
-                        nc.tensor.transpose(flipped[:, g, u, :], x_sorted[:, k, g, u, :], masked_ident[:, k, :])
-                if first == 0:
-                    keep_warm(1)
-                grouped = stage.tile([P, PASSES, P, PACK], BF16, align_bytes=64)
-                nc.scalar.copy(out=grouped[:].bitcast(F32), in_=flipped[:].rearrange("p g u n -> p g n u"))
-                group_tiles.append(grouped)
-            for k, grouped in zip(range(first, first + GROUP), group_tiles):
-                nc.vector.quantize_mx(
-                    out=x_codes[:, k].rearrange("p g n -> p (g n)").bitcast(FP8X4),
-                    scales=x_scales[:, k].rearrange("p g n -> p (g n)"),
-                    in_=grouped[:].rearrange("p g n t -> p (g n t)"),
-                )
+            staged[BY_TENSOR + v] = grouped
+
+        def quantise(k):
+            nc.vector.quantize_mx(
+                out=x_codes[:, k].rearrange("p g n -> p (g n)").bitcast(FP8X4),
+                scales=x_scales[:, k].rearrange("p g n -> p (g n)"),
+                in_=staged[k][:].rearrange("p g n t -> p (g n t)"),
+            )
 
         def multiply_edge(k, n):
             for g in range(PASSES):
@@ -165,44 +197,31 @@ def tile_declayerj_pb_kernel(tc, h2, h_V, mask_attend, W3_w_words, W3_w_scales, 
             for k in range(first, first + GROUP):
                 multiply_edge(k, n)
 
-        transpose_and_quantise(0)
-        for first in range(GROUP, BY_TENSOR, GROUP):
-            multiply(first - GROUP, 0)
-            transpose_and_quantise(first)
-            multiply(first - GROUP, 1)
-
-        nc.vector.tensor_copy(out=mask_a[:], in_=mask_a_bf[:])
+        for k in range(0, GROUP):
+            flip_on_tensor(k)
+        for k in range(0, GROUP):
+            quantise(k)
+        nc.vector.tensor_copy(out=mask_a[:], in_=picked[:])
+        multiply(0, 0)
+        for k in range(GROUP, 2 * GROUP):
+            flip_on_tensor(k)
+        for k in range(GROUP, 2 * GROUP):
+            quantise(k)
+        multiply(0, 1)
+        multiply(GROUP, 0)
+        for k in range(2 * GROUP, BY_TENSOR):
+            flip_on_tensor(k)
+        for k in range(2 * GROUP, BY_TENSOR):
+            quantise(k)
+        multiply(GROUP, 1)
         for v in range(BY_VECTOR):
-            for b in range(QUADRANTS):
-                nc.scalar.activation(
-                    out=a1[:, v, b].rearrange("p (u i h) -> p u i h", u=HALVES, h=2),
-                    in_=a0[:, b, v].rearrange("p (i u h) -> p u i h", u=HALVES, h=2),
-                    func=COPY,
-                    scale=mask_a[:, b, BY_TENSOR + v : BY_TENSOR + v + 1],
-                )
-
-        def flip_blocks(v):
-            nc.vector.transpose(out=t1[:, v, :], in_=a1[:, v].rearrange("p b c -> p (b c)").bitcast(F32))
-
+            mask_and_sort(v)
         flip_blocks(0)
         for v in range(BY_VECTOR):
-            k = BY_TENSOR + v
-            grouped = stage.tile([P, PASSES, P, PACK], BF16, align_bytes=64)
-            for g in range(PASSES):
-                nc.vector.tensor_copy(
-                    out=grouped[:, g]
-                    .rearrange("p n t -> p (n t)")
-                    .bitcast(F32)
-                    .rearrange("p (b j u) -> p b j u", b=QUADRANTS, u=HALVES),
-                    in_=t1[:, v].rearrange("p (b u g j) -> p g b j u", b=QUADRANTS, u=HALVES, g=PASSES)[:, g],
-                )
+            interleave(v, nc.vector.tensor_copy)
             if v + 1 < BY_VECTOR:
                 flip_blocks(v + 1)
-            nc.vector.quantize_mx(
-                out=x_codes[:, k].rearrange("p g n -> p (g n)").bitcast(FP8X4),
-                scales=x_scales[:, k].rearrange("p g n -> p (g n)"),
-                in_=grouped[:].rearrange("p g n t -> p (g n t)"),
-            )
+            quantise(BY_TENSOR + v)
 
         nc.vector.tensor_reduce(out=kept_edges[:], in_=mask[:], axis=mybir.AxisListType.X, op=ADD)
         nc.vector.tensor_scalar(out=bias_weight[:], in0=kept_edges[:], scalar1=1.0 / SCALE, scalar2=None, op0=MULT)

@@ -25,7 +25,7 @@ HALVES = 2
 N_TILE = 512
 N_TILES = H_OUT // N_TILE
 GROUP = 4
-WARM_FIRST = 6
+WARM_FIRST = 3
 BY_VECTOR = 4
 BY_TENSOR = EDGES - BY_VECTOR
 QUADRANTS = 4

@@ -150,8 +150,8 @@ def tile_declayerj_pb_kernel(tc, h2, h_V, mask_attend, W3_w_words, W3_w_scales, 
             nc.scalar.copy(out=grouped[:].bitcast(F32), in_=flipped[:].rearrange("p g u n -> p g n u"))
             staged[k] = grouped
 
-        def mask_and_sort(v):
-            for b in range(QUADRANTS):
+        def mask_and_sort(v, blocks):
+            for b in blocks:
                 nc.scalar.activation(
                     out=a1[:, v, b].rearrange("p (u i h) -> p u i h", u=HALVES, h=2),
                     in_=a0[:, b, v].rearrange("p (i u h) -> p u i h", u=HALVES, h=2),
@@ -208,6 +208,8 @@ def tile_declayerj_pb_kernel(tc, h2, h_V, mask_attend, W3_w_words, W3_w_scales, 
         for k in range(GROUP, 2 * GROUP):
             quantise(k)
         multiply(0, 1)
+        for v in range(BY_VECTOR):
+            mask_and_sort(v, range(0, 1))
         multiply(GROUP, 0)
         for k in range(2 * GROUP, BY_TENSOR):
             flip_on_tensor(k)
@@ -215,7 +217,7 @@ def tile_declayerj_pb_kernel(tc, h2, h_V, mask_attend, W3_w_words, W3_w_scales, 
             quantise(k)
         multiply(GROUP, 1)
         for v in range(BY_VECTOR):
-            mask_and_sort(v)
+            mask_and_sort(v, range(1, QUADRANTS))
         flip_blocks(0)
         for v in range(BY_VECTOR):
             interleave(v, nc.vector.tensor_copy)

@@ -24,11 +24,14 @@ PASSES = M_IN // K_PASS
 HALVES = 2
 N_TILE = 512
 N_TILES = H_OUT // N_TILE
-GROUP = 4
+GROUPS = (4, 4, 4)
+FIRST = GROUPS[0]
 WARM_FIRST = 3
 BY_VECTOR = 4
 BY_TENSOR = EDGES - BY_VECTOR
+EDGES_OF = [range(sum(GROUPS[:i]), sum(GROUPS[: i + 1])) for i in range(len(GROUPS))]
 QUADRANTS = 4
+UNSORTED = FIRST
 Q = P // QUADRANTS
 COPY = mybir.ActivationFunctionType.Copy
 
@@ -44,10 +47,9 @@ def tile_declayerj_pb_kernel(tc, h2, h_V, mask_attend, W3_w_words, W3_w_scales, 
 
     with ExitStack() as ctx:
         keep = ctx.enter_context(tc.tile_pool(name="keep", bufs=1))
-        stage = ctx.enter_context(tc.tile_pool(name="stage", bufs=2 * GROUP))
+        stage = ctx.enter_context(tc.tile_pool(name="stage", bufs=EDGES - BY_VECTOR))
         sums = ctx.enter_context(tc.psum_pool(name="sums", bufs=1))
-        flips = ctx.enter_context(tc.psum_pool(name="flips", bufs=5))
-        spare = ctx.enter_context(tc.psum_pool(name="spare", bufs=1))
+        flips = ctx.enter_context(tc.psum_pool(name="flips", bufs=6))
         ctx.enter_context(tc.manual_schedule())
 
         mask = keep.tile([P, EDGES], BF16)
@@ -57,13 +59,13 @@ def tile_declayerj_pb_kernel(tc, h2, h_V, mask_attend, W3_w_words, W3_w_scales, 
         t1 = keep.tile([P, BY_VECTOR, QUADRANTS * PASSES * Q * HALVES], F32, align_bytes=64)
         mask_a = keep.tile([P, QUADRANTS, EDGES], F32)
         pick = keep.tile([P, QUADRANTS, QUADRANTS, Q], BF16)
-        w_words = keep.tile([P, N_TILES, PASSES, 2 * N_TILE], U8, align_bytes=64)
-        w_scales = keep.tile([P, PASSES, H_OUT], U8, align_bytes=64)
+        w_words = keep.tile([P, N_TILES, PASSES, 2 * N_TILE], U8, align_bytes=256)
+        w_scales = keep.tile([P, PASSES, H_OUT], U8, align_bytes=256)
         ident = keep.tile([P, P], F32)
         masked_ident = keep.tile([P, EDGES, P], F32)
         x_sorted = keep.tile([P, EDGES, PASSES, HALVES, P], F32)
-        x_codes = keep.tile([P, EDGES, PASSES, P], U32, align_bytes=64)
-        x_scales = keep.tile([P, EDGES, PASSES, P], U8, align_bytes=64)
+        x_codes = keep.tile([P, EDGES, PASSES, P], U32, align_bytes=256)
+        x_scales = keep.tile([P, EDGES, PASSES, P], U8, align_bytes=256)
         hv = keep.tile([P, H_OUT], BF16)
         bias = keep.tile([P, H_OUT], BF16)
         kept_edges = keep.tile([P, 1], F32)
@@ -72,13 +74,12 @@ def tile_declayerj_pb_kernel(tc, h2, h_V, mask_attend, W3_w_words, W3_w_scales, 
         result = keep.tile([P, H_OUT], F32)
         acc = [sums.tile([P, N_TILE], F32, name="acc%d" % n) for n in range(N_TILES)]
         zeros = keep.tile([P, N_TILE], BF16)
-        unread = spare.tile([P, N_TILE], F32)
 
         nc.vector.memset(zeros[:], 0.0)
 
         def keep_warm(count):
             for i in range(count):
-                nc.tensor.matmul(out=unread[:], lhsT=zeros[:, 0:P], rhs=zeros[:], start=True, stop=True)
+                nc.tensor.matmul(out=acc[1][:], lhsT=zeros[:, 0:P], rhs=zeros[:], start=True, stop=True)
 
         keep_warm(WARM_FIRST)
 
@@ -105,25 +106,25 @@ def tile_declayerj_pb_kernel(tc, h2, h_V, mask_attend, W3_w_words, W3_w_scales, 
                 )
 
         nc.sync.dma_start(out=mask[:], in_=mask_by_node)
-        load_edges(0, GROUP)
+        load_edges(0, FIRST)
         for quadrant in range(4):
             nc.sync.dma_start(
                 out=w_scales[32 * quadrant : 32 * quadrant + 4, :, :].bitcast(I32),
                 in_=W3_w_scales.bitcast(I32)[:, 4 * quadrant : 4 * quadrant + 4, :].rearrange("g r n -> r g n"),
             )
         load_weight_half(0)
-        load_edges(GROUP, 2 * GROUP)
+        load_edges(FIRST, EDGES_OF[2][0])
         load_weight_half(1)
         pieces = [(b, q) for b in range(QUADRANTS) for q in (0, 2, 1, 3)]
         load_by_quadrant(pieces[:QUADRANTS])
-        load_edges(2 * GROUP, BY_TENSOR)
+        load_edges(EDGES_OF[2][0], BY_TENSOR)
         load_by_quadrant(pieces[QUADRANTS:])
         nc.sync.dma_start(out=hv[:], in_=hv_by_node)
         nc.sync.dma_start(out=bias[:], in_=W3_b.partition_broadcast(P))
 
         for q in range(QUADRANTS):
             nc.vector.tensor_copy(out=pick[:, :, q, :], in_=ident[:].rearrange("p (b j) -> p b j", b=QUADRANTS))
-        picked = flips.tile([P, QUADRANTS, EDGES], F32, name="flipped")
+        picked = acc[0][:, 0 : QUADRANTS * EDGES].rearrange("p (b k) -> p b k", b=QUADRANTS)
         for b in range(QUADRANTS):
             nc.tensor.matmul(
                 out=picked[:, b, :], lhsT=pick[:, b].rearrange("p q j -> p (q j)"), rhs=mask[:], start=True, stop=True
@@ -132,22 +133,31 @@ def tile_declayerj_pb_kernel(tc, h2, h_V, mask_attend, W3_w_words, W3_w_scales, 
         x_words = x[:].bitcast(F32)
         staged = {}
 
-        def flip_on_tensor(k):
+        def mask_identity(k):
             nc.vector.tensor_scalar(
                 out=masked_ident[:, k, :], in0=ident[:], scalar1=mask[:, k : k + 1], scalar2=None, op0=MULT
             )
-            nc.vector.tensor_copy(
-                out=x_sorted[:, k],
-                in_=x_words[:, k, :].rearrange("p (g q u) -> p g u q", g=PASSES, u=HALVES),
-            )
+
+        def words_of(k):
+            return x_words[:, k, :].rearrange("p (g q u) -> p g u q", g=PASSES, u=HALVES)
+
+        def sort_words(k):
+            nc.vector.tensor_copy(out=x_sorted[:, k], in_=words_of(k))
+
+        def passes_at_once(k):
+            return [slice(g, g + 1) for g in range(PASSES)] if k == 0 else [slice(0, PASSES)]
+
+        def flip_on_tensor(k):
+            words = words_of(k) if k < UNSORTED else x_sorted[:, k]
             flipped = flips.tile([P, PASSES, HALVES, P], F32)
             for g in range(PASSES):
                 for u in range(HALVES):
-                    nc.tensor.transpose(flipped[:, g, u, :], x_sorted[:, k, g, u, :], masked_ident[:, k, :])
-            if k < GROUP:
+                    nc.tensor.transpose(flipped[:, g, u, :], words[:, g, u, :], masked_ident[:, k, :])
+            if k < FIRST - 1:
                 keep_warm(1)
             grouped = stage.tile([P, PASSES, P, PACK], BF16, align_bytes=64)
-            nc.scalar.copy(out=grouped[:].bitcast(F32), in_=flipped[:].rearrange("p g u n -> p g n u"))
+            for gs in passes_at_once(k):
+                nc.scalar.copy(out=grouped[:, gs].bitcast(F32), in_=flipped[:, gs].rearrange("p g u n -> p g n u"))
             staged[k] = grouped
 
         def mask_and_sort(v, blocks):
@@ -175,11 +185,12 @@ def tile_declayerj_pb_kernel(tc, h2, h_V, mask_attend, W3_w_words, W3_w_scales, 
             staged[BY_TENSOR + v] = grouped
 
         def quantise(k):
-            nc.vector.quantize_mx(
-                out=x_codes[:, k].rearrange("p g n -> p (g n)").bitcast(FP8X4),
-                scales=x_scales[:, k].rearrange("p g n -> p (g n)"),
-                in_=staged[k][:].rearrange("p g n t -> p (g n t)"),
-            )
+            for gs in passes_at_once(k):
+                nc.vector.quantize_mx(
+                    out=x_codes[:, k, gs].rearrange("p g n -> p (g n)").bitcast(FP8X4),
+                    scales=x_scales[:, k, gs].rearrange("p g n -> p (g n)"),
+                    in_=staged[k][:, gs].rearrange("p g n t -> p (g n t)"),
+                )
 
         def multiply_edge(k, n):
             for g in range(PASSES):
@@ -193,29 +204,36 @@ def tile_declayerj_pb_kernel(tc, h2, h_V, mask_attend, W3_w_words, W3_w_scales, 
                     stop=(k == EDGES - 1 and g == PASSES - 1),
                 )
 
-        def multiply(first, n):
-            for k in range(first, first + GROUP):
+        def flip_group(group):
+            for k in EDGES_OF[group]:
+                if k >= UNSORTED:
+                    mask_identity(k)
+                    sort_words(k)
+                flip_on_tensor(k)
+
+        def quantise_group(group):
+            for k in EDGES_OF[group]:
+                quantise(k)
+
+        def multiply(group, n):
+            for k in EDGES_OF[group]:
                 multiply_edge(k, n)
 
-        for k in range(0, GROUP):
-            flip_on_tensor(k)
-        for k in range(0, GROUP):
-            quantise(k)
-        nc.vector.tensor_copy(out=mask_a[:], in_=picked[:])
+        for k in range(UNSORTED):
+            mask_identity(k)
+        nc.vector.tensor_copy(out=mask_a[:], in_=picked)
+        flip_group(0)
+        quantise_group(0)
         multiply(0, 0)
-        for k in range(GROUP, 2 * GROUP):
-            flip_on_tensor(k)
-        for k in range(GROUP, 2 * GROUP):
-            quantise(k)
+        flip_group(1)
+        quantise_group(1)
         multiply(0, 1)
         for v in range(BY_VECTOR):
             mask_and_sort(v, range(0, 1))
-        multiply(GROUP, 0)
-        for k in range(2 * GROUP, BY_TENSOR):
-            flip_on_tensor(k)
-        for k in range(2 * GROUP, BY_TENSOR):
-            quantise(k)
-        multiply(GROUP, 1)
+        multiply(1, 0)
+        flip_group(2)
+        quantise_group(2)
+        multiply(1, 1)
         for v in range(BY_VECTOR):
             mask_and_sort(v, range(1, QUADRANTS))
         flip_blocks(0)
@@ -231,8 +249,8 @@ def tile_declayerj_pb_kernel(tc, h2, h_V, mask_attend, W3_w_words, W3_w_scales, 
             out=base[:], in0=bias[:], scalar=bias_weight[:, 0:1], in1=hv[:], op0=MULT, op1=ADD
         )
 
-        multiply(BY_TENSOR - GROUP, 0)
-        multiply(BY_TENSOR - GROUP, 1)
+        multiply(2, 0)
+        multiply(2, 1)
         for k in range(BY_TENSOR, EDGES - 2):
             for n in range(N_TILES):
                 multiply_edge(k, n)
@@ -240,9 +258,9 @@ def tile_declayerj_pb_kernel(tc, h2, h_V, mask_attend, W3_w_words, W3_w_scales, 
             for k in range(EDGES - 2, EDGES):
                 multiply_edge(k, n)
 
-        for n in range(N_TILES):
-            cols = slice(N_TILE * n, N_TILE * (n + 1))
+        for n, first, last in ((0, 0, N_TILE), (1, 0, N_TILE // 2), (1, N_TILE // 2, N_TILE)):
+            cols = slice(N_TILE * n + first, N_TILE * n + last)
             nc.vector.scalar_tensor_tensor(
-                out=result[:, cols], in0=acc[n][:], scalar=1.0 / SCALE, in1=base[:, cols], op0=MULT, op1=ADD
+                out=result[:, cols], in0=acc[n][:, first:last], scalar=1.0 / SCALE, in1=base[:, cols], op0=MULT, op1=ADD
             )
             nc.sync.dma_start(out=out_by_node[:, cols], in_=result[:, cols])

from contextlib import ExitStack

import concourse.mybir as mybir
from concourse.masks import make_identity

F32 = mybir.dt.float32
BF16 = mybir.dt.bfloat16
I32 = mybir.dt.int32
U32 = mybir.dt.uint32
U8 = mybir.dt.uint8
FP8X4 = mybir.dt.float8_e4m3fn_x4
FP4X4 = mybir.dt.float4_e2m1fn_x4
MULT = mybir.AluOpType.mult
ADD = mybir.AluOpType.add

P = 128
EDGES = 16
M_IN = 1024
H_OUT = 1024
SCALE = 30.0
PACK = 4
K_PASS = P * PACK
PASSES = M_IN // K_PASS
HALVES = 2
N_TILE = 512
N_TILES = H_OUT // N_TILE
GROUPS = (4, 4, 4)
FIRST = GROUPS[0]
WARM_FIRST = 3
BY_VECTOR = 4
BY_TENSOR = EDGES - BY_VECTOR
EDGES_OF = [range(sum(GROUPS[:i]), sum(GROUPS[: i + 1])) for i in range(len(GROUPS))]
QUADRANTS = 4
UNSORTED = FIRST
Q = P // QUADRANTS
COPY = mybir.ActivationFunctionType.Copy

FLOPS = 2 * P * EDGES * M_IN * H_OUT


def tile_declayerj_pb_kernel(tc, h2, h_V, mask_attend, W3_w_words, W3_w_scales, W3_b, out):
    nc = tc.nc
    h2_by_node = h2.rearrange("b n k m -> (b n) k m")
    mask_by_node = mask_attend.rearrange("b n k -> (b n) k")
    hv_by_node = h_V.rearrange("b n h -> (b n) h")
    out_by_node = out.rearrange("b n h -> (b n) h")

    with ExitStack() as ctx:
        keep = ctx.enter_context(tc.tile_pool(name="keep", bufs=1))
        stage = ctx.enter_context(tc.tile_pool(name="stage", bufs=EDGES - BY_VECTOR))
        sums = ctx.enter_context(tc.psum_pool(name="sums", bufs=1))
        flips = ctx.enter_context(tc.psum_pool(name="flips", bufs=6))
        ctx.enter_context(tc.manual_schedule())

        mask = keep.tile([P, EDGES], BF16)
        x = keep.tile([P, BY_TENSOR, M_IN], BF16)
        a0 = keep.tile([P, QUADRANTS, BY_VECTOR, PASSES * Q * PACK], BF16, align_bytes=64)
        a1 = keep.tile([P, BY_VECTOR, QUADRANTS, PASSES * Q * PACK], BF16, align_bytes=64)
        t1 = keep.tile([P, BY_VECTOR, QUADRANTS * PASSES * Q * HALVES], F32, align_bytes=64)
        mask_a = keep.tile([P, QUADRANTS, EDGES], F32)
        pick = keep.tile([P, QUADRANTS, QUADRANTS, Q], BF16)
        w_words = keep.tile([P, N_TILES, PASSES, 2 * N_TILE], U8, align_bytes=256)
        w_scales = keep.tile([P, PASSES, H_OUT], U8, align_bytes=256)
        ident = keep.tile([P, P], F32)
        masked_ident = keep.tile([P, EDGES, P], F32)
        x_sorted = keep.tile([P, EDGES, PASSES, HALVES, P], F32)
        x_codes = keep.tile([P, EDGES, PASSES, P], U32, align_bytes=256)
        x_scales = keep.tile([P, EDGES, PASSES, P], U8, align_bytes=256)
        hv = keep.tile([P, H_OUT], BF16)
        bias = keep.tile([P, H_OUT], BF16)
        kept_edges = keep.tile([P, 1], F32)
        bias_weight = keep.tile([P, 1], F32)
        base = keep.tile([P, H_OUT], F32)
        result = keep.tile([P, H_OUT], F32)
        acc = [sums.tile([P, N_TILE], F32, name="acc%d" % n) for n in range(N_TILES)]
        zeros = keep.tile([P, N_TILE], BF16)

        nc.vector.memset(zeros[:], 0.0)

        def keep_warm(count):
            for i in range(count):
                nc.tensor.matmul(out=acc[1][:], lhsT=zeros[:, 0:P], rhs=zeros[:], start=True, stop=True)

        keep_warm(WARM_FIRST)

        nc.vector.memset(w_scales[:].rearrange("p g n -> p (g n)").bitcast(I32), 0)
        make_identity(nc, ident[:])

        def load_edges(first, last):
            for k in range(first, last):
                nc.sync.dma_start(out=x[:, k, :], in_=h2_by_node[:, k, :])

        def load_weight_half(n):
            nc.sync.dma_start(
                out=w_words[:, n].bitcast(I32),
                in_=W3_w_words.bitcast(I32)[:, :, N_TILE // 2 * n : N_TILE // 2 * (n + 1)].rearrange("g p b -> p g b"),
            )

        def load_by_quadrant(pieces):
            for b, q in pieces:
                nc.sync.dma_start(
                    out=a0[Q * q : Q * (q + 1), b].rearrange("p v (g w) -> p (v g) w", g=PASSES),
                    in_=h2_by_node[Q * b : Q * (b + 1), BY_TENSOR:EDGES, :].rearrange(
                        "n v (g q w) -> n (v g) q w", g=PASSES, q=QUADRANTS
                    )[:, :, q, :],
                )

        nc.sync.dma_start(out=mask[:], in_=mask_by_node)
        load_edges(0, FIRST)
        for quadrant in range(4):
            nc.sync.dma_start(
                out=w_scales[32 * quadrant : 32 * quadrant + 4, :, :].bitcast(I32),
                in_=W3_w_scales.bitcast(I32)[:, 4 * quadrant : 4 * quadrant + 4, :].rearrange("g r n -> r g n"),
            )
        load_weight_half(0)
        load_edges(FIRST, EDGES_OF[2][0])
        load_weight_half(1)
        pieces = [(b, q) for b in range(QUADRANTS) for q in (0, 2, 1, 3)]
        load_by_quadrant(pieces[:QUADRANTS])
        load_edges(EDGES_OF[2][0], BY_TENSOR)
        load_by_quadrant(pieces[QUADRANTS:])
        nc.sync.dma_start(out=hv[:], in_=hv_by_node)
        nc.sync.dma_start(out=bias[:], in_=W3_b.partition_broadcast(P))

        for q in range(QUADRANTS):
            nc.vector.tensor_copy(out=pick[:, :, q, :], in_=ident[:].rearrange("p (b j) -> p b j", b=QUADRANTS))
        picked = acc[0][:, 0 : QUADRANTS * EDGES].rearrange("p (b k) -> p b k", b=QUADRANTS)
        for b in range(QUADRANTS):
            nc.tensor.matmul(
                out=picked[:, b, :], lhsT=pick[:, b].rearrange("p q j -> p (q j)"), rhs=mask[:], start=True, stop=True
            )

        x_words = x[:].bitcast(F32)
        staged = {}

        def mask_identity(k):
            nc.vector.tensor_scalar(
                out=masked_ident[:, k, :], in0=ident[:], scalar1=mask[:, k : k + 1], scalar2=None, op0=MULT
            )

        def words_of(k):
            return x_words[:, k, :].rearrange("p (g q u) -> p g u q", g=PASSES, u=HALVES)

        def sort_words(k):
            nc.vector.tensor_copy(out=x_sorted[:, k], in_=words_of(k))

        def passes_at_once(k):
            return [slice(g, g + 1) for g in range(PASSES)] if k == 0 else [slice(0, PASSES)]

        def flip_on_tensor(k):
            words = words_of(k) if k < UNSORTED else x_sorted[:, k]
            flipped = flips.tile([P, PASSES, HALVES, P], F32)
            for g in range(PASSES):
                for u in range(HALVES):
                    nc.tensor.transpose(flipped[:, g, u, :], words[:, g, u, :], masked_ident[:, k, :])
            if k < FIRST - 1:
                keep_warm(1)
            grouped = stage.tile([P, PASSES, P, PACK], BF16, align_bytes=64)
            for gs in passes_at_once(k):
                nc.scalar.copy(out=grouped[:, gs].bitcast(F32), in_=flipped[:, gs].rearrange("p g u n -> p g n u"))
            staged[k] = grouped

        def mask_and_sort(v, blocks):
            for b in blocks:
                nc.scalar.activation(
                    out=a1[:, v, b].rearrange("p (u i h) -> p u i h", u=HALVES, h=2),
                    in_=a0[:, b, v].rearrange("p (i u h) -> p u i h", u=HALVES, h=2),
                    func=COPY,
                    scale=mask_a[:, b, BY_TENSOR + v : BY_TENSOR + v + 1],
                )

        def flip_blocks(v):
            nc.vector.transpose(out=t1[:, v, :], in_=a1[:, v].rearrange("p b c -> p (b c)").bitcast(F32))

        def interleave(v, copy):
            grouped = stage.tile([P, PASSES, P, PACK], BF16, align_bytes=64)
            for g in range(PASSES):
                copy(
                    out=grouped[:, g]
                    .rearrange("p n t -> p (n t)")
                    .bitcast(F32)
                    .rearrange("p (b j u) -> p b j u", b=QUADRANTS, u=HALVES),
                    in_=t1[:, v].rearrange("p (b u g j) -> p g b j u", b=QUADRANTS, u=HALVES, g=PASSES)[:, g],
                )
            staged[BY_TENSOR + v] = grouped

        def quantise(k):
            for gs in passes_at_once(k):
                nc.vector.quantize_mx(
                    out=x_codes[:, k, gs].rearrange("p g n -> p (g n)").bitcast(FP8X4),
                    scales=x_scales[:, k, gs].rearrange("p g n -> p (g n)"),
                    in_=staged[k][:, gs].rearrange("p g n t -> p (g n t)"),
                )

        def multiply_edge(k, n):
            for g in range(PASSES):
                nc.tensor.matmul_mx(
                    out=acc[n][:],
                    lhsT=x_codes[:, k, g, :].bitcast(FP8X4),
                    lhsT_scale=x_scales[:, k, g, :],
                    rhs=w_words[:, n, g, :].bitcast(FP4X4),
                    rhs_scale=w_scales[:, g, N_TILE * n : N_TILE * (n + 1)],
                    start=(k == 0 and g == 0),
                    stop=(k == EDGES - 1 and g == PASSES - 1),
                )

        def flip_group(group):
            for k in EDGES_OF[group]:
                if k >= UNSORTED:
                    mask_identity(k)
                    sort_words(k)
                flip_on_tensor(k)

        def quantise_group(group):
            for k in EDGES_OF[group]:
                quantise(k)

        def multiply(group, n):
            for k in EDGES_OF[group]:
                multiply_edge(k, n)

        for k in range(UNSORTED):
            mask_identity(k)
        nc.vector.tensor_copy(out=mask_a[:], in_=picked)
        flip_group(0)
        quantise_group(0)
        multiply(0, 0)
        flip_group(1)
        quantise_group(1)
        multiply(0, 1)
        for v in range(BY_VECTOR):
            mask_and_sort(v, range(0, 1))
        multiply(1, 0)
        flip_group(2)
        quantise_group(2)
        multiply(1, 1)
        for v in range(BY_VECTOR):
            mask_and_sort(v, range(1, QUADRANTS))
        flip_blocks(0)
        for v in range(BY_VECTOR):
            interleave(v, nc.vector.tensor_copy)
            if v + 1 < BY_VECTOR:
                flip_blocks(v + 1)
            quantise(BY_TENSOR + v)

        nc.vector.tensor_reduce(out=kept_edges[:], in_=mask[:], axis=mybir.AxisListType.X, op=ADD)
        nc.vector.tensor_scalar(out=bias_weight[:], in0=kept_edges[:], scalar1=1.0 / SCALE, scalar2=None, op0=MULT)
        nc.vector.scalar_tensor_tensor(
            out=base[:], in0=bias[:], scalar=bias_weight[:, 0:1], in1=hv[:], op0=MULT, op1=ADD
        )

        multiply(2, 0)
        multiply(2, 1)
        for k in range(BY_TENSOR, EDGES - 2):
            for n in range(N_TILES):
                multiply_edge(k, n)
        for n in range(N_TILES):
            for k in range(EDGES - 2, EDGES):
                multiply_edge(k, n)

        for n, first, last in ((0, 0, N_TILE), (1, 0, N_TILE // 2), (1, N_TILE // 2, N_TILE)):
            cols = slice(N_TILE * n + first, N_TILE * n + last)
            nc.vector.scalar_tensor_tensor(
                out=result[:, cols], in0=acc[n][:, first:last], scalar=1.0 / SCALE, in1=base[:, cols], op0=MULT, op1=ADD
            )
            nc.sync.dma_start(out=out_by_node[:, cols], in_=result[:, cols])
